import numpy as np
import ml_dtypes


def mxq(x, axis, fmt="e4m3"):
    dtype, down = {"e4m3": (ml_dtypes.float8_e4m3fn, 7), "e5m2": (ml_dtypes.float8_e5m2, 14)}[fmt]
    v = np.moveaxis(np.asarray(x, np.float32).astype(ml_dtypes.bfloat16).astype(np.float64), axis, -1)
    blocks = v.reshape(v.shape[:-1] + (-1, 32))
    amax = np.abs(blocks).max(-1, keepdims=True)
    byte = np.maximum(np.where(amax > 0, np.frexp(amax)[1] - 1 + 127, 0) - down, 1)
    scale = np.exp2(byte - 127.0)
    codes = (blocks / scale).astype(np.float32).astype(dtype).astype(np.float64)
    return np.moveaxis((codes * scale).reshape(v.shape), -1, axis)


WIDE = False


def mx_kscale(k):
    if not WIDE:
        return np.ones(k)
    levels = np.array([18, -18])
    if k % 512:
        return np.exp2(np.random.permutation(np.resize(levels, k // 32))).repeat(32)
    a = np.empty((k // 512, 16))
    for p in range(k // 512):
        a[p, :8] = np.random.permutation(np.resize(levels, 8))
        for g in range(8):
            far = levels[np.abs(levels - a[p, g]) >= 10]
            a[p, g + 8] = far[np.random.randint(len(far))]
    return np.exp2(a.ravel()).repeat(32)


BF16 = ml_dtypes.bfloat16


def bf(x):
    return np.asarray(x, np.float32).astype(BF16)


def f64(x):
    return np.asarray(x).astype(np.float64)


B, S, M, H, HD = 2, 512, 1024, 12, 128
T = B * S
E = H * HD


def sigmoid(v):
    return 1.0 / (1.0 + np.exp(-v))


def setup_inputs():
    s = mx_kscale(T).reshape(B, S, 1)
    u = mx_kscale(M)
    v = mx_kscale(E).reshape(H, HD)
    x0 = bf(np.random.standard_normal((B, S, M)))
    wq0 = bf(np.random.standard_normal((M, H, HD)) / np.sqrt(M))
    attn = bf(np.random.standard_normal((B, S, H, HD)) * 0.5)
    wo0 = bf(np.random.standard_normal((H, HD, M)) * 2.0 / np.sqrt(E))
    g = bf(np.random.standard_normal((B, S, M)) * np.exp2(np.random.randint(-6, 1, (B, S, 1))) * 8.0 / s * u)
    gate = (f64(x0).reshape(T, M) @ f64(wq0).reshape(M, E)).reshape(B, S, H, HD)
    return {"hidden_states": bf(f64(x0) * s),
            "Wq_gate": bf(f64(wq0) / v),
            "attn": attn,
            "Wo": bf(f64(wo0) * v[:, :, None] / u),
            "gate": np.asarray(gate, np.float32),
            "grad_out": g}


def reference(hidden_states, Wq_gate, attn, Wo, gate, grad_out):
    sg = sigmoid(f64(gate).reshape(T, E))
    go = f64(grad_out).reshape(T, M)
    wo = f64(Wo).reshape(E, M)
    dg = mxq(go, 1, "e5m2") @ mxq(wo, 1, "e4m3").T
    dz = dg * f64(attn).reshape(T, E) * sg * (1.0 - sg)
    wq = f64(Wq_gate).reshape(M, E)
    x = f64(hidden_states).reshape(T, M)
    dx = mxq(dz, 1, "e5m2") @ mxq(wq, 1, "e4m3").T
    dw = mxq(x, 0, "e4m3").T @ mxq(dz, 0, "e5m2")
    return dx.reshape(B, S, M), dw.reshape(M, H, HD)

from contextlib import ExitStack

import concourse.mybir as mybir
from concourse.masks import make_identity

T, M, E = 1024, 1024, 1536
FLOPS = 3 * 2 * T * M * E
BYTES = 2 * (T * M + M * E + T * E + E * M + T * M) + 4 * T * E + 4 * (T * M + M * E)

F32 = mybir.dt.float32
BF16 = mybir.dt.bfloat16
U32 = mybir.dt.uint32
U8 = mybir.dt.uint8
E4M3 = mybir.dt.float8_e4m3fn_x4
E5M2 = mybir.dt.float8_e5m2_x4
ALU = mybir.AluOpType
ACT = mybir.ActivationFunctionType

P = 128
W = 512


def tile_qwen3_5attention_pb_v_kernel(tc, hidden, wq, attn, wo, gate, gout, dx_out, dw_out):
    nc = tc.nc
    x_v = hidden.rearrange("b s m -> (b s) m").rearrange("(g p j) m -> g p j m", g=2, j=4)
    g_v = gout.rearrange("b s m -> (b s) m").rearrange("(g p j) m -> g p j m", g=2, j=4)
    wq_v = wq.rearrange("m u h -> m (u h)").rearrange("(r b q) e -> r q b e", r=4, q=P)
    wo_v = wo.rearrange("u h m -> (u h) m").rearrange("(c b q) m -> c q b m", c=3, q=P)
    at_v = attn.rearrange("b s u h -> (b s) (u h)").rearrange("(g p j) e -> g p j e", g=2, j=4)
    ga_v = gate.rearrange("b s u h -> (b s) (u h)").rearrange("(g p j) e -> g p j e", g=2, j=4)
    dx_v = dx_out.rearrange("b s m -> (b s) m").rearrange("(g p j) m -> g j p m", g=2, j=4)
    dw_v = dw_out.rearrange("m u h -> m (u h)").rearrange("(t q) e -> t q e", q=P)

    with ExitStack() as ctx:
        keep = ctx.enter_context(tc.tile_pool(name="keep", bufs=1))
        raw = ctx.enter_context(tc.tile_pool(name="raw", bufs=2))
        ewp = ctx.enter_context(tc.tile_pool(name="ewp", bufs=3))
        stage = ctx.enter_context(tc.tile_pool(name="stage", bufs=4))
        stageq = ctx.enter_context(tc.tile_pool(name="stageq", bufs=1))
        stagex = ctx.enter_context(tc.tile_pool(name="stagex", bufs=2))
        mid = ctx.enter_context(tc.tile_pool(name="mid", bufs=2))
        rot = ctx.enter_context(tc.tile_pool(name="rot", bufs=4))
        outp = ctx.enter_context(tc.tile_pool(name="outp", bufs=6))
        ps_dg = ctx.enter_context(tc.psum_pool(name="ps_dg", bufs=2))
        ps_tr = ctx.enter_context(tc.psum_pool(name="ps_tr", bufs=3))
        ps_out = ctx.enter_context(tc.psum_pool(name="ps_out", bufs=3))

        ident = keep.tile([P, P], F32, name="ident")
        make_identity(nc, ident[:])

        def copy(eng, out, in_):
            if eng == "S":
                nc.scalar.copy(out=out, in_=in_)
            else:
                nc.vector.tensor_copy(out=out, in_=in_)

        def new_codes(pool, cols, tag):
            codes = pool.tile([P, cols], U32, name=tag + "_c", align_bytes=64)
            scales = pool.tile([P, cols], U8, name=tag + "_s", align_bytes=64)
            return codes, scales

        def quantize(cs, c0, fmt, src):
            codes, scales = cs
            n = src.shape[1]
            nc.vector.quantize_mx(
                out=codes[:, c0:c0 + n].bitcast(fmt),
                scales=scales[:, c0:c0 + n],
                in_=src.rearrange("p n t -> p (n t)"),
            )

        def turn_bank(blocks, eng, dst):
            bank = ps_tr.tile([P, 2, 2, P], F32, name="bank")
            for i in range(2):
                for u in range(2):
                    nc.tensor.transpose(bank[:, i, u, :], blocks[i][:, u:256:2], ident[:])
            copy(eng, dst.bitcast(F32).rearrange("p (i n) u -> p i n u", i=2), bank[:].rearrange("p i u n -> p i n u"))

        steps = [(c, g) for g in range(2) for c in range(3)]
        gate_t, attn_t, grad_t, wo_t, x_t, wq_t = {}, {}, {}, {}, {}, {}
        gcod, wocod, wqcod, xcod, dzec, dztc, dz_t, grp = {}, {}, {}, {}, {}, {}, {}, {}

        def load_ew(s, parts=1):
            c, g = steps[s]
            ec = slice(W * c, W * c + W)
            gt = ewp.tile([P, 4, W], F32, name="gt", align_bytes=64)
            at = ewp.tile([P, 4, W], BF16, name="at", align_bytes=64)
            n = 4 // parts
            for i in range(parts):
                nc.sync.dma_start(out=gt[:, n * i:n * i + n, :], in_=ga_v[g][:, n * i:n * i + n, ec])
            nc.sync.dma_start(out=at[:], in_=at_v[g][:, :, ec])
            gate_t[s], attn_t[s] = gt, at

        def load_grad(g):
            gr = raw.tile([P, 4, M], BF16, name="gr", align_bytes=64)
            for i in range(2):
                nc.sync.dma_start(out=gr[:, 2 * i:2 * i + 2, :], in_=g_v[g][:, 2 * i:2 * i + 2, :])
            grad_t[g] = gr

        def load_wo(c):
            t = raw.tile([P, 4, M], BF16, name="wor", align_bytes=64)
            for i in range(2):
                nc.sync.dma_start(out=t[:, 2 * i:2 * i + 2, :], in_=wo_v[c][:, 2 * i:2 * i + 2, :])
            wo_t[c] = t

        def load_wq(r):
            t = raw.tile([P, 2, E], BF16, name="wqr", align_bytes=64)
            nc.sync.dma_start(out=t[:], in_=wq_v[r])
            wq_t[r] = t

        def load_x(g):
            t = mid.tile([P, 4, M], BF16, name="xr", align_bytes=64)
            nc.sync.dma_start(out=t[:], in_=x_v[g])
            x_t[g] = t

        def ew(s):
            gt, at = gate_t[s], attn_t[s]

            def act(i, func):
                js = slice(2 * i, 2 * i + 2)
                sc = 0.5 if func == ACT.Tanh else 1.0
                return lambda: nc.scalar.activation(out=gt[:, js, :], in_=gt[:, js, :], func=func, scale=sc)

            def wgt(i):
                js = slice(2 * i, 2 * i + 2)
                return lambda: nc.vector.scalar_tensor_tensor(
                    out=gt[:, js, :], in0=gt[:, js, :], scalar=1.0, in1=at[:, js, :], op0=ALU.subtract, op1=ALU.mult)

            return [act(0, ACT.Tanh), act(0, ACT.Square), act(1, ACT.Tanh), wgt(0), act(1, ACT.Square), wgt(1)]

        def prep(kind, raw_t, cods, key, fmt, engs):
            words = raw_t[:].bitcast(F32)

            def start():
                for h in range(2):
                    cods[key, h] = new_codes(keep, W, "%s%d%d" % (kind, key, h))
                    grp[kind, key, h] = stage.tile([P, W, 4], BF16, name="grouped", align_bytes=64)

            def unit(h, pair, eng):
                return lambda: turn_bank([words[:, 2 * pair + i, 256 * h:256 * h + 256] for i in range(2)], eng,
                                         grp[kind, key, h][:, 256 * pair:256 * pair + 256, :])

            def q(h):
                return lambda: quantize(cods[key, h], 0, fmt, grp[kind, key, h][:])

            def first():
                start()
                unit(0, 0, engs[0])()

            return [first, unit(1, 0, engs[1]), unit(0, 1, engs[2]), unit(1, 1, engs[3]), q(0), q(1)]

        def prep_wq(r, engs):
            words = wq_t[r][:].bitcast(F32)
            n, o = r // 2, 256 * (r % 2)

            def unit(c):
                def run():
                    if r % 2 == 0:
                        wqcod[c, n] = new_codes(keep, W, "wq%d%d" % (c, n))
                        grp["q", c, n] = stageq.tile([P, W, 4], BF16, name="gq%d" % c, align_bytes=64)
                    turn_bank([words[:, i, 256 * c:256 * c + 256] for i in range(2)], engs[c],
                              grp["q", c, n][:, o:o + 256, :])
                return run

            def q(c):
                return lambda: quantize(wqcod[c, n], 0, E4M3, grp["q", c, n][:])

            units = [unit(c) for c in range(3)]
            if r % 2 == 1:
                units = [units[0], units[1], q(0), units[2], q(1), q(2)]
            return units

        def interleave(dst, src):
            nc.vector.tensor_copy(out=dst.rearrange("p (c i) t -> p c t i", i=4),
                                  in_=src.rearrange("p t (c i) -> p c t i", i=4))

        def prep_x(g):
            xcod[g] = new_codes(keep, M, "x%d" % g)
            gx = {}

            def il(i):
                def run():
                    gx[i] = stage.tile([P, W, 4], BF16, name="grouped", align_bytes=64)
                    interleave(gx[i][:], x_t[g][:, :, W * i:W * i + W])
                return run

            def q(i):
                return lambda: quantize(xcod[g], W * i, E4M3, gx[i][:])

            return [il(0), il(1), q(0), q(1)]

        def dg(s):
            c, g = steps[s]
            dz_t[s] = mid.tile([P, 4, W], BF16, name="dz", align_bytes=64)

            def unit(j):
                def run():
                    acc = ps_dg.tile([P, W], F32, name="acc")
                    for h in range(2):
                        gc, gs = gcod[g, h]
                        wc, ws = wocod[c, h]
                        js = slice(P * j, P * j + P)
                        nc.tensor.matmul_mx(out=acc[:], lhsT=gc[:, js].bitcast(E5M2), lhsT_scale=gs[:, js],
                                            rhs=wc[:].bitcast(E4M3), rhs_scale=ws[:], start=h == 0, stop=h == 1)
                    nc.vector.scalar_tensor_tensor(out=dz_t[s][:, j, :], in0=acc[:], scalar=-0.25,
                                                   in1=gate_t[s][:, j, :], op0=ALU.mult, op1=ALU.mult)
                return run

            return [unit(j) for j in range(4)]

        def roads(s, engs):
            c, g = steps[s]
            words = dz_t[s][:].bitcast(F32)
            dzec[c, g] = new_codes(keep, W, "dze%d%d" % (c, g))
            dztc[c, g] = new_codes(keep, W, "dzt%d%d" % (c, g))
            ge = stage.tile([P, W, 4], BF16, name="grouped", align_bytes=64)
            gtok = stage.tile([P, W, 4], BF16, name="grouped", align_bytes=64)

            def unit(pair):
                return lambda: turn_bank([words[:, 2 * pair + i, :] for i in range(2)], engs[pair],
                                         ge[:, 256 * pair:256 * pair + 256, :])

            il = [lambda: interleave(gtok[:], dz_t[s][:])]
            qe = [lambda: quantize(dzec[c, g], 0, E5M2, ge[:])]
            qt = [lambda: quantize(dztc[c, g], 0, E5M2, gtok[:])]
            return [unit(0), unit(1)], il, qe, qt

        def dw(c, engs):
            def unit(t):
                def run():
                    acc = ps_out.tile([P, W], F32, name="oacc")
                    ms = slice(P * t, P * t + P)
                    for g in range(2):
                        xc, xs = xcod[g]
                        zc, zs = dztc[c, g]
                        nc.tensor.matmul_mx(out=acc[:], lhsT=xc[:, ms].bitcast(E4M3), lhsT_scale=xs[:, ms],
                                            rhs=zc[:].bitcast(E5M2), rhs_scale=zs[:], start=g == 0, stop=g == 1)
                    o = outp.tile([P, W], F32, name="dwo")
                    copy(engs[t], o[:], acc[:])
                    nc.sync.dma_start(out=dw_v[t][:, W * c:W * c + W], in_=o[:])
                return run
            return [unit(t) for t in range(8)]

        def dx(g, engs, pools="o"):
            acc = {}

            def passes(j, n, cs):
                js = slice(P * j, P * j + P)
                for c in cs:
                    zc, zs = dzec[c, g]
                    qc, qs = wqcod[c, n]
                    nc.tensor.matmul_mx(out=acc[j, n][:], lhsT=zc[:, js].bitcast(E5M2), lhsT_scale=zs[:, js],
                                        rhs=qc[:].bitcast(E4M3), rhs_scale=qs[:], start=c == 0, stop=c == 2)

            def begin(j, n, where):
                def run():
                    if where == "o":
                        acc[j, n] = ps_out.tile([P, W], F32, name="oacc")
                    else:
                        acc[j, n] = ps_dg.tile([P, W], F32, name="acc")
                    passes(j, n, [0, 1])
                return run

            def finish(j, n):
                def run():
                    passes(j, n, [2])
                    o = outp.tile([P, W], F32, name="dwo")
                    copy(engs[2 * j + n], o[:], acc[j, n][:])
                    nc.sync.dma_start(out=dx_v[g, j][:, W * n:W * n + W], in_=o[:])
                return run

            def both(b, f):
                def run():
                    b()
                    f()
                return run

            jn = [(j, n) for j in range(4) for n in range(2)]
            bs = [begin(j, n, pools[i % len(pools)]) for i, (j, n) in enumerate(jn)]
            fs = [finish(j, n) for j, n in jn]
            return bs, fs, [both(b, f) for b, f in zip(bs, fs)]

        def weave(main, fill):
            out, k = [], 0
            for i, f in enumerate(main):
                out.append(f)
                want = (i + 1) * len(fill) // len(main)
                out += fill[k:want]
                k = want
            return out

        def run(units):
            for f in units:
                f()

        def step(s, early, fill, k, road_engs, nxt):
            d = dg(s)
            n = ew(nxt) if nxt is not None else []
            run(weave(d, early + n[:2]))
            run(fill[:k])
            tr, il, qe, qt = roads(s, road_engs)
            run(tr[:1] + il + tr[1:])
            rest = weave(fill[k:], n[2:]) if len(fill) > k else n[2:]
            cut = min(2, len(rest))
            run(rest[:cut] + qt + qe + rest[cut:])

        for once in range(1):
            load_ew(0, 2)
            load_grad(0)
            load_wo(0)
            load_ew(1)
            load_wo(1)
            load_wq(0)
            load_x(0)
            load_ew(2)
            run(ew(0))
            run(prep("g", grad_t[0], gcod, 0, E5M2, "VVVV"))
            run(prep("w", wo_t[0], wocod, 0, E4M3, "SVSV"))
            load_wo(2)
            load_wq(1)
            step(0, [], prep("w", wo_t[1], wocod, 1, E4M3, "SSSS") + prep_wq(0, "SSS") + prep_x(0), 3, "SS", 1)
            load_grad(1)
            load_wq(2)
            load_ew(3)
            step(1, [], prep("w", wo_t[2], wocod, 2, E4M3, "SSSS") + prep_wq(1, "SSS"), 3, "SS", 2)
            load_wq(3)
            load_x(1)
            load_ew(4)
            step(2, [], prep("g", grad_t[1], gcod, 1, E5M2, "SSSS") + prep_wq(2, "SVS"), 3, "SS", 3)
            load_ew(5)
            x0 = dx(0, "SSSSSSSS")[2]
            step(3, [], prep_wq(3, "SSS") + prep_x(1) + x0[:6], 3, "SS", 4)
            w0 = dw(0, "SSSSSSSS")
            step(4, [], x0[6:] + w0[:6], 3, "SS", 5)
            w1 = dw(1, "SSSVSSSV")
            xb, xf, x1 = dx(1, "SVSVSVSV", "ooodd")
            step(5, [], w0[6:] + w1 + xb[:3], 3, "SV", None)
            w2 = dw(2, "SVSVSVSV")
            run(xf[:3] + weave(x1[3:], w2))
